import numpy as np
import ml_dtypes


def mxq(x, axis, fmt="e4m3"):
    dtype, down = {"e4m3": (ml_dtypes.float8_e4m3fn, 7), "e5m2": (ml_dtypes.float8_e5m2, 14)}[fmt]
    v = np.moveaxis(np.asarray(x, np.float32).astype(ml_dtypes.bfloat16).astype(np.float64), axis, -1)
    blocks = v.reshape(v.shape[:-1] + (-1, 32))
    amax = np.abs(blocks).max(-1, keepdims=True)
    byte = np.maximum(np.where(amax > 0, np.frexp(amax)[1] - 1 + 127, 0) - down, 1)
    scale = np.exp2(byte - 127.0)
    codes = (blocks / scale).astype(np.float32).astype(dtype).astype(np.float64)
    return np.moveaxis((codes * scale).reshape(v.shape), -1, axis)


WIDE = False


def mx_kscale(k):
    if not WIDE:
        return np.ones(k)
    levels = np.array([10, -10, 5, -5, 0])
    a = np.random.permutation(np.resize(levels, k // 512 * 4)).reshape(k // 512, 4)
    idx = np.arange(k)
    return np.exp2(a[idx // 512, idx % 128 // 32])


BF16 = ml_dtypes.bfloat16


def bf(x):
    return np.asarray(x, np.float32).astype(BF16)


def f64(x):
    return np.asarray(x).astype(np.float64)


E2M1 = np.array([0.0, 0.5, 1.0, 1.5, 2.0, 3.0, 4.0, 6.0, -0.0, -0.5, -1.0, -1.5, -2.0, -3.0, -4.0, -6.0])


def pack_weight(w, fmt):
    k, n = w.shape
    w = f64(bf(w)).reshape(k // 32, 32, n)
    amax = np.abs(w).max(1)
    if fmt == "e4m3":
        byte = np.frexp(amax)[1] - 1 + 127 - 7
    else:
        mant, ex = np.frexp(amax / 6.0)
        byte = np.where(mant > 0.5, ex, ex - 1) + 127
    byte = np.clip(np.where(amax > 0, byte, 1), 1, 254)
    scaled = (w * np.exp2(127.0 - byte)[:, None, :]).reshape(k, n).astype(np.float32)
    by_word = np.ascontiguousarray(scaled.reshape(k // 512, 128, 4, n).transpose(0, 1, 3, 2))
    if fmt == "e4m3":
        words = by_word.astype(ml_dtypes.float8_e4m3fn).view(np.uint8)
    else:
        c = by_word.astype(ml_dtypes.float4_e2m1fn).view(np.uint8) & 0xF
        words = c[..., 0::2] | (c[..., 1::2] << 4)
    return np.ascontiguousarray(words), np.ascontiguousarray(byte.astype(np.uint8).reshape(k // 512, 16, n))


def unpack_weight(words, scales, fmt):
    g, p, n, _ = words.shape
    if fmt == "e4m3":
        vals = np.ascontiguousarray(words).view(ml_dtypes.float8_e4m3fn).astype(np.float64)
    else:
        nib = np.empty((g, p, n, 4), np.uint8)
        nib[..., 0::2] = words & 0xF
        nib[..., 1::2] = words >> 4
        vals = E2M1[nib]
    vals = vals * np.repeat(np.exp2(scales.astype(np.float64) - 127.0), 8, axis=1)[..., None]
    return vals.transpose(0, 1, 3, 2).reshape(g * 512, n)


B, C, S, OUT = 128, 4, 64, 1024
IN = C * S * S
HS = S // 2
SUB, BLK = 4, 32


def haar_dwt2_features(x):
    x4 = x.reshape(x.shape[0], C, S, S)
    a = x4[:, :, 0::2, 0::2]
    bq = x4[:, :, 0::2, 1::2]
    c = x4[:, :, 1::2, 0::2]
    d = x4[:, :, 1::2, 1::2]
    LL = (a + bq + c + d) * 0.5
    LH = (a + bq - c - d) * 0.5
    HL = (a - bq + c - d) * 0.5
    HH = (a - bq - c + d) * 0.5
    t = np.stack([LL, LH, HL, HH], axis=2)
    return t.reshape(x.shape[0], -1)


def setup_inputs():
    g = mx_kscale(IN).reshape(-1, SUB, BLK)[:, 0, :].reshape(C, HS, HS)
    gx = np.repeat(np.repeat(g, 2, axis=1), 2, axis=2).reshape(IN)
    gt = np.repeat(g[:, None], SUB, axis=1).reshape(IN)
    x = bf(np.random.standard_normal((B, IN)) * gx)
    w = np.random.standard_normal((OUT, IN)) * (1.0 / np.sqrt(IN)) / gt
    words, scales = pack_weight(np.ascontiguousarray(w.T), "e4m3")
    b = bf(np.random.standard_normal(OUT) * 0.5)
    return {"x": x, "W_words": words, "W_scales": scales, "b": b}


def reference(x, W_words, W_scales, b):
    t = haar_dwt2_features(f64(x))
    return (mxq(t, 1, "e4m3") @ unpack_weight(W_words, W_scales, "e4m3")) + f64(b)

@@ -1,0 +1,156 @@
+from contextlib import ExitStack
+
+import concourse.mybir as mybir
+from concourse.masks import make_identity
+
+BF16 = mybir.dt.bfloat16
+F32 = mybir.dt.float32
+I32 = mybir.dt.int32
+U8 = mybir.dt.uint8
+U32 = mybir.dt.uint32
+FP8X4 = mybir.dt.float8_e4m3fn_x4
+ADD = mybir.AluOpType.add
+SUBTRACT = mybir.AluOpType.subtract
+MULT = mybir.AluOpType.mult
+
+P = 128
+PACK = 4
+CHANNELS = 4
+SUBBANDS = 4
+HALVES = 2
+CHUNKS = CHANNELS * HALVES
+CHUNK_PIXELS = 2048
+PARITY_PIXELS = CHUNK_PIXELS // 2
+ROWS16 = 16
+J8 = 8
+OUT = 1024
+N_TILE = 512
+N_TILES = OUT // N_TILE
+QUADRANTS = 4
+
+FLOPS = 2 * 128 * 16384 * 1024
+
+
+def tile_waveletlinearlayer_k_kernel(tc, x, W_words, W_scales, b, out):
+    nc = tc.nc
+    with ExitStack() as ctx:
+        x_pool = ctx.enter_context(tc.tile_pool(name="x_pool", bufs=CHUNKS))
+        w_pool = ctx.enter_context(tc.tile_pool(name="w_pool", bufs=CHUNKS * SUBBANDS))
+        keep = ctx.enter_context(tc.tile_pool(name="keep", bufs=1))
+        work = ctx.enter_context(tc.tile_pool(name="work", bufs=2))
+        acc_pool = ctx.enter_context(tc.psum_pool(name="acc_pool", bufs=1))
+        bank_pool = ctx.enter_context(tc.psum_pool(name="bank_pool", bufs=3))
+
+        w_planes = keep.tile([P, CHUNKS, OUT], U8, align_bytes=64)
+        nc.vector.memset(w_planes[:].rearrange("p c n -> p (c n)").bitcast(I32), 0)
+
+        x_chunks = []
+        for c in range(CHUNKS):
+            x_chunk = x_pool.tile([P, CHUNK_PIXELS], BF16)
+            nc.sync.dma_start(out=x_chunk[:], in_=x[:, c * CHUNK_PIXELS : (c + 1) * CHUNK_PIXELS])
+            x_chunks.append(x_chunk)
+
+        scale_rows = W_scales.rearrange(
+            "(ch s h) (q r) n -> ch h q s r n", s=SUBBANDS, h=HALVES, q=QUADRANTS
+        )
+        for c in range(CHUNKS):
+            for q in range(QUADRANTS):
+                nc.sync.dma_start(
+                    out=w_planes[32 * q : 32 * q + 16, c, :].bitcast(I32),
+                    in_=scale_rows[c // HALVES, c % HALVES, q].bitcast(I32),
+                )
+
+        w_groups = []
+        for c in range(CHUNKS):
+            for s in range(SUBBANDS):
+                g = (c // HALVES * SUBBANDS + s) * HALVES + c % HALVES
+                w_group = w_pool.tile([P, OUT * PACK], U8, align_bytes=64)
+                nc.sync.dma_start(
+                    out=w_group[:].bitcast(I32),
+                    in_=W_words[g].rearrange("p n t -> p (n t)").bitcast(I32),
+                )
+                w_groups.append(w_group)
+
+        ident = keep.tile([P, P], F32)
+        make_identity(nc, ident[:])
+        ones = keep.tile([P, P], BF16)
+        nc.vector.memset(ones[:], 1.0)
+        bias_rows = keep.tile([P, OUT], BF16)
+        nc.vector.memset(bias_rows[:], 0.0)
+        nc.scalar.dma_start(out=bias_rows[0:1, :], in_=b.rearrange("(o n) -> o n", o=1))
+        bias = keep.tile([P, OUT], F32)
+        for half in range(N_TILES):
+            cols = slice(half * N_TILE, (half + 1) * N_TILE)
+            bias_bank = bank_pool.tile([P, N_TILE], F32, tag="even_rows")
+            nc.tensor.matmul(out=bias_bank[:], lhsT=ones[:], rhs=bias_rows[:, cols], start=True, stop=True)
+            nc.scalar.copy(out=bias[:, cols], in_=bias_bank[:])
+
+        acc = []
+        for half in range(N_TILES):
+            acc_bank = acc_pool.tile([P, N_TILE], F32, name="acc%d" % half)
+            acc.append(acc_bank)
+
+        for c in range(CHUNKS):
+            words = x_chunks[c][:].bitcast(F32).rearrange(
+                "n (i a j t) -> n a t i j", i=ROWS16, a=2, j=J8, t=PACK
+            )
+            sorted_words = work.tile([P, 2, PACK, P], F32)
+            for parity in (1, 0):
+                nc.scalar.copy(
+                    out=sorted_words[:, parity].rearrange("n t (i j) -> n t i j", i=ROWS16),
+                    in_=words[:, parity],
+                )
+
+            odd_rows = bank_pool.tile([P, PACK, P], F32, tag="odd_rows")
+            even_rows = bank_pool.tile([P, PACK, P], F32, tag="even_rows")
+            for t4 in range(PACK):
+                nc.tensor.transpose(out=odd_rows[:, t4, :], in_=sorted_words[:, 1, t4, :], identity=ident[:])
+            for t4 in range(PACK):
+                nc.tensor.transpose(out=even_rows[:, t4, :], in_=sorted_words[:, 0, t4, :], identity=ident[:])
+
+            odd_half = work.tile([P, PARITY_PIXELS], BF16)
+            nc.scalar.mul(
+                out=odd_half[:], in_=odd_rows[:].rearrange("p t n -> p (t n)").bitcast(BF16), mul=0.5
+            )
+
+            even_pixels = even_rows[:].rearrange("p t n -> p (t n)").bitcast(BF16)
+            row_mix = work.tile([P, 2, PARITY_PIXELS], F32)
+            nc.vector.scalar_tensor_tensor(
+                out=row_mix[:, 0, :], in0=even_pixels, scalar=0.5, in1=odd_half[:], op0=MULT, op1=ADD
+            )
+            nc.vector.scalar_tensor_tensor(
+                out=row_mix[:, 1, :], in0=even_pixels, scalar=0.5, in1=odd_half[:], op0=MULT, op1=SUBTRACT
+            )
+
+            pixels = row_mix[:].rearrange("p m (t n e) -> p e m n t", t=PACK, n=P, e=2)
+            features = work.tile([P, SUBBANDS, P, PACK], BF16, align_bytes=64)
+            nc.vector.tensor_tensor(out=features[:, 0:2], in0=pixels[:, 0], in1=pixels[:, 1], op=ADD)
+            nc.vector.tensor_tensor(out=features[:, 2:4], in0=pixels[:, 0], in1=pixels[:, 1], op=SUBTRACT)
+
+            t_codes = work.tile([P, SUBBANDS * P], U32, align_bytes=64)
+            t_scales = work.tile([P, SUBBANDS * P], U8, align_bytes=64)
+            nc.vector.quantize_mx(
+                out=t_codes[:].bitcast(FP8X4),
+                scales=t_scales[:],
+                in_=features[:].rearrange("p s n t -> p (s n t)"),
+            )
+            for s in range(SUBBANDS):
+                batch_cols = slice(s * P, (s + 1) * P)
+                for half in range(N_TILES):
+                    nc.tensor.matmul_mx(
+                        out=acc[half][:],
+                        lhsT=t_codes[:, batch_cols].bitcast(FP8X4),
+                        lhsT_scale=t_scales[:, batch_cols],
+                        rhs=w_groups[c * SUBBANDS + s][
+                            :, half * N_TILE * PACK : (half + 1) * N_TILE * PACK
+                        ].bitcast(FP8X4),
+                        rhs_scale=w_planes[4 * s : P, c, half * N_TILE : (half + 1) * N_TILE],
+                        start=(c == 0 and s == 0),
+                        stop=(c == CHUNKS - 1 and s == SUBBANDS - 1),
+                    )
+
+        result = keep.tile([P, OUT], F32)
+        for half in range(N_TILES):
+            cols = slice(half * N_TILE, (half + 1) * N_TILE)
+            nc.vector.tensor_tensor(out=result[:, cols], in0=acc[half][:], in1=bias[:, cols], op=ADD)
+            nc.sync.dma_start(out=out[:, cols], in_=result[:, cols])

@@ -31,15 +31,21 @@ QUADRANTS = 4
 FLOPS = 2 * 128 * 16384 * 1024
 
 
+LEAD = 3
+
+
 def tile_waveletlinearlayer_k_kernel(tc, x, W_words, W_scales, b, out):
     nc = tc.nc
     with ExitStack() as ctx:
+        ctx.enter_context(tc.manual_schedule())
         x_pool = ctx.enter_context(tc.tile_pool(name="x_pool", bufs=CHUNKS))
         w_pool = ctx.enter_context(tc.tile_pool(name="w_pool", bufs=CHUNKS * SUBBANDS))
         keep = ctx.enter_context(tc.tile_pool(name="keep", bufs=1))
         work = ctx.enter_context(tc.tile_pool(name="work", bufs=2))
+        ahead = ctx.enter_context(tc.tile_pool(name="ahead", bufs=LEAD))
+        coded = ctx.enter_context(tc.tile_pool(name="coded", bufs=4))
         acc_pool = ctx.enter_context(tc.psum_pool(name="acc_pool", bufs=1))
-        bank_pool = ctx.enter_context(tc.psum_pool(name="bank_pool", bufs=3))
+        bank_pool = ctx.enter_context(tc.psum_pool(name="bank_pool", bufs=LEAD))
 
         w_planes = keep.tile([P, CHUNKS, OUT], U8, align_bytes=64)
         nc.vector.memset(w_planes[:].rearrange("p c n -> p (c n)").bitcast(I32), 0)
@@ -78,19 +84,21 @@ def tile_waveletlinearlayer_k_kernel(tc, x, W_words, W_scales, b, out):
         bias_rows = keep.tile([P, OUT], BF16)
         nc.vector.memset(bias_rows[:], 0.0)
         nc.scalar.dma_start(out=bias_rows[0:1, :], in_=b.rearrange("(o n) -> o n", o=1))
-        bias = keep.tile([P, OUT], F32)
-        for half in range(N_TILES):
-            cols = slice(half * N_TILE, (half + 1) * N_TILE)
-            bias_bank = bank_pool.tile([P, N_TILE], F32, tag="even_rows")
-            nc.tensor.matmul(out=bias_bank[:], lhsT=ones[:], rhs=bias_rows[:, cols], start=True, stop=True)
-            nc.scalar.copy(out=bias[:, cols], in_=bias_bank[:])
 
         acc = []
         for half in range(N_TILES):
             acc_bank = acc_pool.tile([P, N_TILE], F32, name="acc%d" % half)
             acc.append(acc_bank)
 
-        for c in range(CHUNKS):
+        sorted_of = {}
+        odd_bank_of = {}
+        even_bank_of = {}
+        odd_half_of = {}
+        row_mix_of = {}
+        codes_of = {}
+        scales_of = {}
+
+        def sort_and_transpose(c):
             words = x_chunks[c][:].bitcast(F32).rearrange(
                 "n (i a j t) -> n a t i j", i=ROWS16, a=2, j=J8, t=PACK
             )
@@ -100,47 +108,58 @@ def tile_waveletlinearlayer_k_kernel(tc, x, W_words, W_scales, b, out):
                     out=sorted_words[:, parity].rearrange("n t (i j) -> n t i j", i=ROWS16),
                     in_=words[:, parity],
                 )
-
             odd_rows = bank_pool.tile([P, PACK, P], F32, tag="odd_rows")
             even_rows = bank_pool.tile([P, PACK, P], F32, tag="even_rows")
             for t4 in range(PACK):
                 nc.tensor.transpose(out=odd_rows[:, t4, :], in_=sorted_words[:, 1, t4, :], identity=ident[:])
             for t4 in range(PACK):
                 nc.tensor.transpose(out=even_rows[:, t4, :], in_=sorted_words[:, 0, t4, :], identity=ident[:])
+            odd_bank_of[c] = odd_rows
+            even_bank_of[c] = even_rows
 
-            odd_half = work.tile([P, PARITY_PIXELS], BF16)
+        def halve_odd_rows(c):
+            odd_half = ahead.tile([P, PARITY_PIXELS], BF16)
             nc.scalar.mul(
-                out=odd_half[:], in_=odd_rows[:].rearrange("p t n -> p (t n)").bitcast(BF16), mul=0.5
+                out=odd_half[:], in_=odd_bank_of[c][:].rearrange("p t n -> p (t n)").bitcast(BF16), mul=0.5
             )
+            odd_half_of[c] = odd_half
 
-            even_pixels = even_rows[:].rearrange("p t n -> p (t n)").bitcast(BF16)
+        def mix_rows(c):
+            even_pixels = even_bank_of[c][:].rearrange("p t n -> p (t n)").bitcast(BF16)
             row_mix = work.tile([P, 2, PARITY_PIXELS], F32)
             nc.vector.scalar_tensor_tensor(
-                out=row_mix[:, 0, :], in0=even_pixels, scalar=0.5, in1=odd_half[:], op0=MULT, op1=ADD
+                out=row_mix[:, 0, :], in0=even_pixels, scalar=0.5, in1=odd_half_of[c][:], op0=MULT, op1=ADD
             )
             nc.vector.scalar_tensor_tensor(
-                out=row_mix[:, 1, :], in0=even_pixels, scalar=0.5, in1=odd_half[:], op0=MULT, op1=SUBTRACT
+                out=row_mix[:, 1, :], in0=even_pixels, scalar=0.5, in1=odd_half_of[c][:], op0=MULT, op1=SUBTRACT
             )
+            row_mix_of[c] = row_mix
 
-            pixels = row_mix[:].rearrange("p m (t n e) -> p e m n t", t=PACK, n=P, e=2)
-            features = work.tile([P, SUBBANDS, P, PACK], BF16, align_bytes=64)
-            nc.vector.tensor_tensor(out=features[:, 0:2], in0=pixels[:, 0], in1=pixels[:, 1], op=ADD)
-            nc.vector.tensor_tensor(out=features[:, 2:4], in0=pixels[:, 0], in1=pixels[:, 1], op=SUBTRACT)
+        def mix_columns_and_quantise(c):
+            pixels = row_mix_of[c][:].rearrange("p m (t n e) -> p e m n t", t=PACK, n=P, e=2)
+            sums = work.tile([P, 2, P, PACK], BF16, align_bytes=64)
+            differences = work.tile([P, 2, P, PACK], BF16, align_bytes=64)
+            nc.vector.tensor_tensor(out=sums[:], in0=pixels[:, 0], in1=pixels[:, 1], op=ADD)
+            nc.vector.tensor_tensor(out=differences[:], in0=pixels[:, 0], in1=pixels[:, 1], op=SUBTRACT)
+            for pair, features in enumerate((sums, differences)):
+                t_codes = coded.tile([P, 2 * P], U32, align_bytes=64, name="t_codes%d" % pair)
+                t_scales = coded.tile([P, 2 * P], U8, align_bytes=64, name="t_scales%d" % pair)
+                nc.vector.quantize_mx(
+                    out=t_codes[:].bitcast(FP8X4),
+                    scales=t_scales[:],
+                    in_=features[:].rearrange("p m n t -> p (m n t)"),
+                )
+                codes_of[(c, pair)] = t_codes
+                scales_of[(c, pair)] = t_scales
 
-            t_codes = work.tile([P, SUBBANDS * P], U32, align_bytes=64)
-            t_scales = work.tile([P, SUBBANDS * P], U8, align_bytes=64)
-            nc.vector.quantize_mx(
-                out=t_codes[:].bitcast(FP8X4),
-                scales=t_scales[:],
-                in_=features[:].rearrange("p s n t -> p (s n t)"),
-            )
+        def multiply(c):
             for s in range(SUBBANDS):
-                batch_cols = slice(s * P, (s + 1) * P)
+                batch_cols = slice(s % 2 * P, (s % 2 + 1) * P)
                 for half in range(N_TILES):
                     nc.tensor.matmul_mx(
                         out=acc[half][:],
-                        lhsT=t_codes[:, batch_cols].bitcast(FP8X4),
-                        lhsT_scale=t_scales[:, batch_cols],
+                        lhsT=codes_of[(c, s // 2)][:, batch_cols].bitcast(FP8X4),
+                        lhsT_scale=scales_of[(c, s // 2)][:, batch_cols],
                         rhs=w_groups[c * SUBBANDS + s][
                             :, half * N_TILE * PACK : (half + 1) * N_TILE * PACK
                         ].bitcast(FP8X4),
@@ -148,6 +167,30 @@ def tile_waveletlinearlayer_k_kernel(tc, x, W_words, W_scales, b, out):
                         start=(c == 0 and s == 0),
                         stop=(c == CHUNKS - 1 and s == SUBBANDS - 1),
                     )
+
+        for c in range(LEAD):
+            sort_and_transpose(c)
+        for c in range(LEAD - 1):
+            halve_odd_rows(c)
+        for c in range(CHUNKS):
+            mix_rows(c)
+            if c + LEAD < CHUNKS:
+                sort_and_transpose(c + LEAD)
+            if c + LEAD - 1 < CHUNKS:
+                halve_odd_rows(c + LEAD - 1)
+            if c >= 1:
+                mix_columns_and_quantise(c - 1)
+                multiply(c - 1)
+
+        bias = keep.tile([P, OUT], F32)
+        for half in range(N_TILES):
+            cols = slice(half * N_TILE, (half + 1) * N_TILE)
+            bias_bank = bank_pool.tile([P, N_TILE], F32, tag="even_rows")
+            nc.tensor.matmul(out=bias_bank[:], lhsT=ones[:], rhs=bias_rows[:, cols], start=True, stop=True)
+            nc.scalar.copy(out=bias[:, cols], in_=bias_bank[:])
+
+        mix_columns_and_quantise(CHUNKS - 1)
+        multiply(CHUNKS - 1)
 
         result = keep.tile([P, OUT], F32)
         for half in range(N_TILES):

@@ -108,24 +108,24 @@ def tile_waveletlinearlayer_k_kernel(tc, x, W_words, W_scales, b, out):
                     out=sorted_words[:, parity].rearrange("n t (i j) -> n t i j", i=ROWS16),
                     in_=words[:, parity],
                 )
-            odd_rows = bank_pool.tile([P, PACK, P], F32, tag="odd_rows")
-            even_rows = bank_pool.tile([P, PACK, P], F32, tag="even_rows")
+            odd_rows = bank_pool.tile([P, P, PACK], F32, tag="odd_rows")
+            even_rows = bank_pool.tile([P, P, PACK], F32, tag="even_rows")
             for t4 in range(PACK):
-                nc.tensor.transpose(out=odd_rows[:, t4, :], in_=sorted_words[:, 1, t4, :], identity=ident[:])
+                nc.tensor.transpose(out=odd_rows[:, :, t4], in_=sorted_words[:, 1, t4, :], identity=ident[:])
             for t4 in range(PACK):
-                nc.tensor.transpose(out=even_rows[:, t4, :], in_=sorted_words[:, 0, t4, :], identity=ident[:])
+                nc.tensor.transpose(out=even_rows[:, :, t4], in_=sorted_words[:, 0, t4, :], identity=ident[:])
             odd_bank_of[c] = odd_rows
             even_bank_of[c] = even_rows
 
         def halve_odd_rows(c):
             odd_half = ahead.tile([P, PARITY_PIXELS], BF16)
             nc.scalar.mul(
-                out=odd_half[:], in_=odd_bank_of[c][:].rearrange("p t n -> p (t n)").bitcast(BF16), mul=0.5
+                out=odd_half[:], in_=odd_bank_of[c][:].rearrange("p n t -> p (n t)").bitcast(BF16), mul=0.5
             )
             odd_half_of[c] = odd_half
 
         def mix_rows(c):
-            even_pixels = even_bank_of[c][:].rearrange("p t n -> p (t n)").bitcast(BF16)
+            even_pixels = even_bank_of[c][:].rearrange("p n t -> p (n t)").bitcast(BF16)
             row_mix = work.tile([P, 2, PARITY_PIXELS], F32)
             nc.vector.scalar_tensor_tensor(
                 out=row_mix[:, 0, :], in0=even_pixels, scalar=0.5, in1=odd_half_of[c][:], op0=MULT, op1=ADD
@@ -136,7 +136,7 @@ def tile_waveletlinearlayer_k_kernel(tc, x, W_words, W_scales, b, out):
             row_mix_of[c] = row_mix
 
         def mix_columns_and_quantise(c):
-            pixels = row_mix_of[c][:].rearrange("p m (t n e) -> p e m n t", t=PACK, n=P, e=2)
+            pixels = row_mix_of[c][:].rearrange("p m (n t e) -> p e m n t", t=PACK, n=P, e=2)
             sums = work.tile([P, 2, P, PACK], BF16, align_bytes=64)
             differences = work.tile([P, 2, P, PACK], BF16, align_bytes=64)
             nc.vector.tensor_tensor(out=sums[:], in0=pixels[:, 0], in1=pixels[:, 1], op=ADD)

@@ -38,8 +38,8 @@ def tile_waveletlinearlayer_k_kernel(tc, x, W_words, W_scales, b, out):
     nc = tc.nc
     with ExitStack() as ctx:
         ctx.enter_context(tc.manual_schedule())
-        x_pool = ctx.enter_context(tc.tile_pool(name="x_pool", bufs=CHUNKS))
-        w_pool = ctx.enter_context(tc.tile_pool(name="w_pool", bufs=CHUNKS * SUBBANDS))
+        x_pool = ctx.enter_context(tc.tile_pool(name="x_pool", bufs=CHANNELS))
+        w_pool = ctx.enter_context(tc.tile_pool(name="w_pool", bufs=CHUNKS))
         keep = ctx.enter_context(tc.tile_pool(name="keep", bufs=1))
         work = ctx.enter_context(tc.tile_pool(name="work", bufs=2))
         ahead = ctx.enter_context(tc.tile_pool(name="ahead", bufs=LEAD))
@@ -51,10 +51,17 @@ def tile_waveletlinearlayer_k_kernel(tc, x, W_words, W_scales, b, out):
         nc.vector.memset(w_planes[:].rearrange("p c n -> p (c n)").bitcast(I32), 0)
 
         x_chunks = []
-        for c in range(CHUNKS):
-            x_chunk = x_pool.tile([P, CHUNK_PIXELS], BF16)
-            nc.sync.dma_start(out=x_chunk[:], in_=x[:, c * CHUNK_PIXELS : (c + 1) * CHUNK_PIXELS])
-            x_chunks.append(x_chunk)
+        for ch in range(CHANNELS):
+            x_channel = x_pool.tile([P, HALVES * CHUNK_PIXELS], BF16)
+            pieces = HALVES if ch == 0 else 1
+            width = HALVES * CHUNK_PIXELS // pieces
+            for piece in range(pieces):
+                nc.sync.dma_start(
+                    out=x_channel[:, piece * width : (piece + 1) * width],
+                    in_=x[:, ch * HALVES * CHUNK_PIXELS + piece * width : ch * HALVES * CHUNK_PIXELS + (piece + 1) * width],
+                )
+            for h in range(HALVES):
+                x_chunks.append(x_channel[:, h * CHUNK_PIXELS : (h + 1) * CHUNK_PIXELS])
 
         scale_rows = W_scales.rearrange(
             "(ch s h) (q r) n -> ch h q s r n", s=SUBBANDS, h=HALVES, q=QUADRANTS
@@ -66,16 +73,18 @@ def tile_waveletlinearlayer_k_kernel(tc, x, W_words, W_scales, b, out):
                     in_=scale_rows[c // HALVES, c % HALVES, q].bitcast(I32),
                 )
 
+        chunk_words = W_words.rearrange("(ch s h) p n t -> ch h p s (n t)", s=SUBBANDS, h=HALVES)
         w_groups = []
         for c in range(CHUNKS):
-            for s in range(SUBBANDS):
-                g = (c // HALVES * SUBBANDS + s) * HALVES + c % HALVES
-                w_group = w_pool.tile([P, OUT * PACK], U8, align_bytes=64)
+            w_chunk = w_pool.tile([P, SUBBANDS, OUT * PACK], U8, align_bytes=64)
+            together = 1 if c == CHUNKS - 1 else 2
+            for s in range(0, SUBBANDS, together):
                 nc.sync.dma_start(
-                    out=w_group[:].bitcast(I32),
-                    in_=W_words[g].rearrange("p n t -> p (n t)").bitcast(I32),
+                    out=w_chunk[:, s : s + together, :].bitcast(I32),
+                    in_=chunk_words[c // HALVES, c % HALVES][:, s : s + together, :].bitcast(I32),
                 )
-                w_groups.append(w_group)
+            for s in range(SUBBANDS):
+                w_groups.append(w_chunk[:, s, :])
 
         ident = keep.tile([P, P], F32)
         make_identity(nc, ident[:])
@@ -99,7 +108,7 @@ def tile_waveletlinearlayer_k_kernel(tc, x, W_words, W_scales, b, out):
         scales_of = {}
 
         def sort_and_transpose(c):
-            words = x_chunks[c][:].bitcast(F32).rearrange(
+            words = x_chunks[c].bitcast(F32).rearrange(
                 "n (i a j t) -> n a t i j", i=ROWS16, a=2, j=J8, t=PACK
             )
             sorted_words = work.tile([P, 2, PACK, P], F32)

@@ -47,6 +47,11 @@ def tile_waveletlinearlayer_k_kernel(tc, x, W_words, W_scales, b, out):
         acc_pool = ctx.enter_context(tc.psum_pool(name="acc_pool", bufs=1))
         bank_pool = ctx.enter_context(tc.psum_pool(name="bank_pool", bufs=LEAD))
 
+        warm_in = keep.tile([P, 1], F32)
+        warm_out = keep.tile([P, 1], F32)
+        nc.vector.memset(warm_in[:], 0.0)
+        nc.scalar.mul(out=warm_out[:], in_=warm_in[:], mul=0.5)
+
         w_planes = keep.tile([P, CHUNKS, OUT], U8, align_bytes=64)
         nc.vector.memset(w_planes[:].rearrange("p c n -> p (c n)").bitcast(I32), 0)
 
@@ -179,8 +184,8 @@ def tile_waveletlinearlayer_k_kernel(tc, x, W_words, W_scales, b, out):
 
         for c in range(LEAD):
             sort_and_transpose(c)
-        for c in range(LEAD - 1):
-            halve_odd_rows(c)
+            if c < LEAD - 1:
+                halve_odd_rows(c)
         for c in range(CHUNKS):
             mix_rows(c)
             if c + LEAD < CHUNKS:

@@ -52,6 +52,9 @@ def tile_waveletlinearlayer_k_kernel(tc, x, W_words, W_scales, b, out):
         nc.vector.memset(warm_in[:], 0.0)
         nc.scalar.mul(out=warm_out[:], in_=warm_in[:], mul=0.5)
 
+        ident = keep.tile([P, P], F32)
+        make_identity(nc, ident[:])
+
         w_planes = keep.tile([P, CHUNKS, OUT], U8, align_bytes=64)
         nc.vector.memset(w_planes[:].rearrange("p c n -> p (c n)").bitcast(I32), 0)
 
@@ -73,9 +76,9 @@ def tile_waveletlinearlayer_k_kernel(tc, x, W_words, W_scales, b, out):
         )
         for c in range(CHUNKS):
             for q in range(QUADRANTS):
-                nc.sync.dma_start(
-                    out=w_planes[32 * q : 32 * q + 16, c, :].bitcast(I32),
-                    in_=scale_rows[c // HALVES, c % HALVES, q].bitcast(I32),
+                nc.gpsimd.dma_start(
+                    out=w_planes[32 * q : 32 * q + 16, c, :].bitcast(F32),
+                    in_=scale_rows[c // HALVES, c % HALVES, q].bitcast(F32),
                 )
 
         chunk_words = W_words.rearrange("(ch s h) p n t -> ch h p s (n t)", s=SUBBANDS, h=HALVES)
@@ -91,8 +94,6 @@ def tile_waveletlinearlayer_k_kernel(tc, x, W_words, W_scales, b, out):
             for s in range(SUBBANDS):
                 w_groups.append(w_chunk[:, s, :])
 
-        ident = keep.tile([P, P], F32)
-        make_identity(nc, ident[:])
         ones = keep.tile([P, P], BF16)
         nc.vector.memset(ones[:], 1.0)
         bias_rows = keep.tile([P, OUT], BF16)

@@ -32,6 +32,7 @@ FLOPS = 2 * 128 * 16384 * 1024
 
 
 LEAD = 3
+LAST = CHUNKS - 1
 
 
 def tile_waveletlinearlayer_k_kernel(tc, x, W_words, W_scales, b, out):
@@ -94,6 +95,10 @@ def tile_waveletlinearlayer_k_kernel(tc, x, W_words, W_scales, b, out):
             for s in range(SUBBANDS):
                 w_groups.append(w_chunk[:, s, :])
 
+        plus_half = keep.tile([P, P], BF16)
+        nc.vector.tensor_scalar_mul(out=plus_half[:], in0=ident[:], scalar1=0.5)
+        minus_half = keep.tile([P, P], BF16)
+        nc.vector.tensor_scalar_mul(out=minus_half[:], in0=ident[:], scalar1=-0.5)
         ones = keep.tile([P, P], BF16)
         nc.vector.memset(ones[:], 1.0)
         bias_rows = keep.tile([P, OUT], BF16)
@@ -157,15 +162,38 @@ def tile_waveletlinearlayer_k_kernel(tc, x, W_words, W_scales, b, out):
             nc.vector.tensor_tensor(out=sums[:], in0=pixels[:, 0], in1=pixels[:, 1], op=ADD)
             nc.vector.tensor_tensor(out=differences[:], in0=pixels[:, 0], in1=pixels[:, 1], op=SUBTRACT)
             for pair, features in enumerate((sums, differences)):
-                t_codes = coded.tile([P, 2 * P], U32, align_bytes=64, name="t_codes%d" % pair)
-                t_scales = coded.tile([P, 2 * P], U8, align_bytes=64, name="t_scales%d" % pair)
-                nc.vector.quantize_mx(
-                    out=t_codes[:].bitcast(FP8X4),
-                    scales=t_scales[:],
-                    in_=features[:].rearrange("p m n t -> p (m n t)"),
+                quantise(c, pair, features[:].rearrange("p m n t -> p (m n t)"))
+
+        def quantise(c, pair, features):
+            t_codes = coded.tile([P, 2 * P], U32, align_bytes=64, name="t_codes%d" % pair)
+            t_scales = coded.tile([P, 2 * P], U8, align_bytes=64, name="t_scales%d" % pair)
+            nc.vector.quantize_mx(out=t_codes[:].bitcast(FP8X4), scales=t_scales[:], in_=features)
+            codes_of[(c, pair)] = t_codes
+            scales_of[(c, pair)] = t_scales
+
+        last_pixels = keep.tile([P, 2, PARITY_PIXELS], BF16)
+        last_features = keep.tile([P, SUBBANDS, N_TILE], BF16, align_bytes=64)
+
+        def fetch_pixels(c):
+            for parity, bank in ((1, odd_bank_of[c]), (0, even_bank_of[c])):
+                nc.scalar.copy(
+                    out=last_pixels[:, parity, :], in_=bank[:].rearrange("p n t -> p (n t)").bitcast(BF16)
                 )
-                codes_of[(c, pair)] = t_codes
-                scales_of[(c, pair)] = t_scales
+
+        def transform(pair):
+            for s, tag in ((2 * pair, "odd_rows"), (2 * pair + 1, "even_rows")):
+                feature_bank = bank_pool.tile([P, N_TILE], F32, tag=tag)
+                for a in range(2):
+                    for e in range(2):
+                        negative = (a * (s % 2) + e * (s // 2)) % 2 == 1
+                        nc.tensor.matmul(
+                            out=feature_bank[:],
+                            lhsT=(minus_half if negative else plus_half)[:],
+                            rhs=last_pixels[:, a, :].rearrange("p (w e) -> p e w", e=2)[:, e, :],
+                            start=(a == 0 and e == 0),
+                            stop=(a == 1 and e == 1),
+                        )
+                nc.scalar.copy(out=last_features[:, s, :], in_=feature_bank[:])
 
         def multiply(c):
             for s in range(SUBBANDS):
@@ -187,12 +215,16 @@ def tile_waveletlinearlayer_k_kernel(tc, x, W_words, W_scales, b, out):
             sort_and_transpose(c)
             if c < LEAD - 1:
                 halve_odd_rows(c)
-        for c in range(CHUNKS):
+        for c in range(LAST):
             mix_rows(c)
             if c + LEAD < CHUNKS:
                 sort_and_transpose(c + LEAD)
-            if c + LEAD - 1 < CHUNKS:
+            if c + LEAD - 1 < LAST:
                 halve_odd_rows(c + LEAD - 1)
+            if c + LEAD == LAST:
+                fetch_pixels(LAST)
+            if c >= LAST - 2:
+                transform(c - (LAST - 2))
             if c >= 1:
                 mix_columns_and_quantise(c - 1)
                 multiply(c - 1)
@@ -204,8 +236,11 @@ def tile_waveletlinearlayer_k_kernel(tc, x, W_words, W_scales, b, out):
             nc.tensor.matmul(out=bias_bank[:], lhsT=ones[:], rhs=bias_rows[:, cols], start=True, stop=True)
             nc.scalar.copy(out=bias[:, cols], in_=bias_bank[:])
 
-        mix_columns_and_quantise(CHUNKS - 1)
-        multiply(CHUNKS - 1)
+        mix_columns_and_quantise(LAST - 1)
+        multiply(LAST - 1)
+        for pair in range(2):
+            quantise(LAST, pair, last_features[:, 2 * pair : 2 * pair + 2, :].rearrange("p m c -> p (m c)"))
+        multiply(LAST)
 
         result = keep.tile([P, OUT], F32)
         for half in range(N_TILES):

@@ -83,14 +83,23 @@ def tile_waveletlinearlayer_k_kernel(tc, x, W_words, W_scales, b, out):
                 )
 
         chunk_words = W_words.rearrange("(ch s h) p n t -> ch h p s (n t)", s=SUBBANDS, h=HALVES)
+        half_bytes = N_TILE * PACK
         w_groups = []
         for c in range(CHUNKS):
             w_chunk = w_pool.tile([P, SUBBANDS, OUT * PACK], U8, align_bytes=64)
-            together = 1 if c == CHUNKS - 1 else 2
-            for s in range(0, SUBBANDS, together):
+            if c < CHUNKS - 1:
+                pieces = ((0, 2, 0, 2 * half_bytes), (2, 4, 0, 2 * half_bytes))
+            else:
+                pieces = (
+                    (0, 4, 0, half_bytes),
+                    (0, 2, half_bytes, 2 * half_bytes),
+                    (2, 3, half_bytes, 2 * half_bytes),
+                    (3, 4, half_bytes, 2 * half_bytes),
+                )
+            for s0, s1, b0, b1 in pieces:
                 nc.sync.dma_start(
-                    out=w_chunk[:, s : s + together, :].bitcast(I32),
-                    in_=chunk_words[c // HALVES, c % HALVES][:, s : s + together, :].bitcast(I32),
+                    out=w_chunk[:, s0:s1, b0:b1].bitcast(I32),
+                    in_=chunk_words[c // HALVES, c % HALVES][:, s0:s1, b0:b1].bitcast(I32),
                 )
             for s in range(SUBBANDS):
                 w_groups.append(w_chunk[:, s, :])
@@ -195,21 +204,22 @@ def tile_waveletlinearlayer_k_kernel(tc, x, W_words, W_scales, b, out):
                         )
                 nc.scalar.copy(out=last_features[:, s, :], in_=feature_bank[:])
 
+        def one_pass(c, s, half):
+            batch_cols = slice(s % 2 * P, (s % 2 + 1) * P)
+            nc.tensor.matmul_mx(
+                out=acc[half][:],
+                lhsT=codes_of[(c, s // 2)][:, batch_cols].bitcast(FP8X4),
+                lhsT_scale=scales_of[(c, s // 2)][:, batch_cols],
+                rhs=w_groups[c * SUBBANDS + s][:, half * N_TILE * PACK : (half + 1) * N_TILE * PACK].bitcast(FP8X4),
+                rhs_scale=w_planes[4 * s : P, c, half * N_TILE : (half + 1) * N_TILE],
+                start=(c == 0 and s == 0),
+                stop=(c == CHUNKS - 1 and s == SUBBANDS - 1),
+            )
+
         def multiply(c):
             for s in range(SUBBANDS):
-                batch_cols = slice(s % 2 * P, (s % 2 + 1) * P)
                 for half in range(N_TILES):
-                    nc.tensor.matmul_mx(
-                        out=acc[half][:],
-                        lhsT=codes_of[(c, s // 2)][:, batch_cols].bitcast(FP8X4),
-                        lhsT_scale=scales_of[(c, s // 2)][:, batch_cols],
-                        rhs=w_groups[c * SUBBANDS + s][
-                            :, half * N_TILE * PACK : (half + 1) * N_TILE * PACK
-                        ].bitcast(FP8X4),
-                        rhs_scale=w_planes[4 * s : P, c, half * N_TILE : (half + 1) * N_TILE],
-                        start=(c == 0 and s == 0),
-                        stop=(c == CHUNKS - 1 and s == SUBBANDS - 1),
-                    )
+                    one_pass(c, s, half)
 
         for c in range(LEAD):
             sort_and_transpose(c)
@@ -240,10 +250,11 @@ def tile_waveletlinearlayer_k_kernel(tc, x, W_words, W_scales, b, out):
         multiply(LAST - 1)
         for pair in range(2):
             quantise(LAST, pair, last_features[:, 2 * pair : 2 * pair + 2, :].rearrange("p m c -> p (m c)"))
-        multiply(LAST)
 
         result = keep.tile([P, OUT], F32)
         for half in range(N_TILES):
+            for s in range(SUBBANDS):
+                one_pass(LAST, s, half)
             cols = slice(half * N_TILE, (half + 1) * N_TILE)
             nc.vector.tensor_tensor(out=result[:, cols], in0=acc[half][:], in1=bias[:, cols], op=ADD)
             nc.sync.dma_start(out=out[:, cols], in_=result[:, cols])

@@ -26,6 +26,7 @@ J8 = 8
 OUT = 1024
 N_TILE = 512
 N_TILES = OUT // N_TILE
+QUARTER = OUT // 4
 QUADRANTS = 4
 
 FLOPS = 2 * 128 * 16384 * 1024
@@ -39,7 +40,6 @@ def tile_waveletlinearlayer_k_kernel(tc, x, W_words, W_scales, b, out):
     nc = tc.nc
     with ExitStack() as ctx:
         ctx.enter_context(tc.manual_schedule())
-        x_pool = ctx.enter_context(tc.tile_pool(name="x_pool", bufs=CHANNELS))
         w_pool = ctx.enter_context(tc.tile_pool(name="w_pool", bufs=CHUNKS))
         keep = ctx.enter_context(tc.tile_pool(name="keep", bufs=1))
         work = ctx.enter_context(tc.tile_pool(name="work", bufs=2))
@@ -60,17 +60,12 @@ def tile_waveletlinearlayer_k_kernel(tc, x, W_words, W_scales, b, out):
         nc.vector.memset(w_planes[:].rearrange("p c n -> p (c n)").bitcast(I32), 0)
 
         x_chunks = []
-        for ch in range(CHANNELS):
-            x_channel = x_pool.tile([P, HALVES * CHUNK_PIXELS], BF16)
-            pieces = HALVES if ch == 0 else 1
-            width = HALVES * CHUNK_PIXELS // pieces
-            for piece in range(pieces):
-                nc.sync.dma_start(
-                    out=x_channel[:, piece * width : (piece + 1) * width],
-                    in_=x[:, ch * HALVES * CHUNK_PIXELS + piece * width : ch * HALVES * CHUNK_PIXELS + (piece + 1) * width],
-                )
-            for h in range(HALVES):
-                x_chunks.append(x_channel[:, h * CHUNK_PIXELS : (h + 1) * CHUNK_PIXELS])
+        x_all = keep.tile([P, CHUNKS * CHUNK_PIXELS], BF16)
+        for c0, c1 in ((0, 1), (1, 4), (4, 8)):
+            pixels = slice(c0 * CHUNK_PIXELS, c1 * CHUNK_PIXELS)
+            nc.sync.dma_start(out=x_all[:, pixels], in_=x[:, pixels])
+        for c in range(CHUNKS):
+            x_chunks.append(x_all[:, c * CHUNK_PIXELS : (c + 1) * CHUNK_PIXELS])
 
         scale_rows = W_scales.rearrange(
             "(ch s h) (q r) n -> ch h q s r n", s=SUBBANDS, h=HALVES, q=QUADRANTS
@@ -94,7 +89,8 @@ def tile_waveletlinearlayer_k_kernel(tc, x, W_words, W_scales, b, out):
                     (0, 4, 0, half_bytes),
                     (0, 2, half_bytes, 2 * half_bytes),
                     (2, 3, half_bytes, 2 * half_bytes),
-                    (3, 4, half_bytes, 2 * half_bytes),
+                    (3, 4, half_bytes, 3 * half_bytes // 2),
+                    (3, 4, 3 * half_bytes // 2, 2 * half_bytes),
                 )
             for s0, s1, b0, b1 in pieces:
                 nc.sync.dma_start(
@@ -204,6 +200,20 @@ def tile_waveletlinearlayer_k_kernel(tc, x, W_words, W_scales, b, out):
                         )
                 nc.scalar.copy(out=last_features[:, s, :], in_=feature_bank[:])
 
+        def last_pass(s, quarter, bank):
+            batch_cols = slice(s % 2 * P, (s % 2 + 1) * P)
+            nc.tensor.matmul_mx(
+                out=bank[:],
+                lhsT=codes_of[(LAST, s // 2)][:, batch_cols].bitcast(FP8X4),
+                lhsT_scale=scales_of[(LAST, s // 2)][:, batch_cols],
+                rhs=w_groups[LAST * SUBBANDS + s][
+                    :, quarter * QUARTER * PACK : (quarter + 1) * QUARTER * PACK
+                ].bitcast(FP8X4),
+                rhs_scale=w_planes[4 * s : P, LAST, quarter * QUARTER : (quarter + 1) * QUARTER],
+                start=(s == 0),
+                stop=(s == SUBBANDS - 1),
+            )
+
         def one_pass(c, s, half):
             batch_cols = slice(s % 2 * P, (s % 2 + 1) * P)
             nc.tensor.matmul_mx(
@@ -213,7 +223,7 @@ def tile_waveletlinearlayer_k_kernel(tc, x, W_words, W_scales, b, out):
                 rhs=w_groups[c * SUBBANDS + s][:, half * N_TILE * PACK : (half + 1) * N_TILE * PACK].bitcast(FP8X4),
                 rhs_scale=w_planes[4 * s : P, c, half * N_TILE : (half + 1) * N_TILE],
                 start=(c == 0 and s == 0),
-                stop=(c == CHUNKS - 1 and s == SUBBANDS - 1),
+                stop=(c == CHUNKS - 1 - half and s == SUBBANDS - 1),
             )
 
         def multiply(c):
@@ -252,9 +262,23 @@ def tile_waveletlinearlayer_k_kernel(tc, x, W_words, W_scales, b, out):
             quantise(LAST, pair, last_features[:, 2 * pair : 2 * pair + 2, :].rearrange("p m c -> p (m c)"))
 
         result = keep.tile([P, OUT], F32)
-        for half in range(N_TILES):
-            for s in range(SUBBANDS):
-                one_pass(LAST, s, half)
-            cols = slice(half * N_TILE, (half + 1) * N_TILE)
-            nc.vector.tensor_tensor(out=result[:, cols], in0=acc[half][:], in1=bias[:, cols], op=ADD)
+        so_far = keep.tile([P, N_TILE], F32)
+        first, second = slice(0, N_TILE), slice(N_TILE, OUT)
+        nc.vector.tensor_tensor(out=so_far[:], in0=acc[1][:], in1=bias[:, second], op=ADD)
+        for s in range(SUBBANDS):
+            one_pass(LAST, s, 0)
+        nc.vector.tensor_tensor(out=result[:, first], in0=acc[0][:], in1=bias[:, first], op=ADD)
+        nc.sync.dma_start(out=out[:, first], in_=result[:, first])
+        quarters = []
+        for tag in ("odd_rows", "even_rows"):
+            quarter_bank = bank_pool.tile([P, QUARTER], F32, tag=tag)
+            quarters.append(quarter_bank)
+        for s in range(SUBBANDS):
+            for i, bank in enumerate(quarters):
+                last_pass(s, 2 + i, bank)
+        for i, bank in enumerate(quarters):
+            cols = slice((2 + i) * QUARTER, (3 + i) * QUARTER)
+            nc.vector.tensor_tensor(
+                out=result[:, cols], in0=bank[:], in1=so_far[:, i * QUARTER : (i + 1) * QUARTER], op=ADD
+            )
             nc.sync.dma_start(out=out[:, cols], in_=result[:, cols])

@@ -26,7 +26,6 @@ J8 = 8
 OUT = 1024
 N_TILE = 512
 N_TILES = OUT // N_TILE
-QUARTER = OUT // 4
 QUADRANTS = 4
 
 FLOPS = 2 * 128 * 16384 * 1024
@@ -83,14 +82,15 @@ def tile_waveletlinearlayer_k_kernel(tc, x, W_words, W_scales, b, out):
         for c in range(CHUNKS):
             w_chunk = w_pool.tile([P, SUBBANDS, OUT * PACK], U8, align_bytes=64)
             if c < CHUNKS - 1:
-                pieces = ((0, 2, 0, 2 * half_bytes), (2, 4, 0, 2 * half_bytes))
+                pieces = ((0, 4, 0, 2 * half_bytes),)
             else:
                 pieces = (
                     (0, 4, 0, half_bytes),
                     (0, 2, half_bytes, 2 * half_bytes),
                     (2, 3, half_bytes, 2 * half_bytes),
                     (3, 4, half_bytes, 3 * half_bytes // 2),
-                    (3, 4, 3 * half_bytes // 2, 2 * half_bytes),
+                    (3, 4, 3 * half_bytes // 2, 7 * half_bytes // 4),
+                    (3, 4, 7 * half_bytes // 4, 2 * half_bytes),
                 )
             for s0, s1, b0, b1 in pieces:
                 nc.sync.dma_start(
@@ -200,16 +200,14 @@ def tile_waveletlinearlayer_k_kernel(tc, x, W_words, W_scales, b, out):
                         )
                 nc.scalar.copy(out=last_features[:, s, :], in_=feature_bank[:])
 
-        def last_pass(s, quarter, bank):
+        def last_pass(s, n0, n1, bank):
             batch_cols = slice(s % 2 * P, (s % 2 + 1) * P)
             nc.tensor.matmul_mx(
                 out=bank[:],
                 lhsT=codes_of[(LAST, s // 2)][:, batch_cols].bitcast(FP8X4),
                 lhsT_scale=scales_of[(LAST, s // 2)][:, batch_cols],
-                rhs=w_groups[LAST * SUBBANDS + s][
-                    :, quarter * QUARTER * PACK : (quarter + 1) * QUARTER * PACK
-                ].bitcast(FP8X4),
-                rhs_scale=w_planes[4 * s : P, LAST, quarter * QUARTER : (quarter + 1) * QUARTER],
+                rhs=w_groups[LAST * SUBBANDS + s][:, n0 * PACK : n1 * PACK].bitcast(FP8X4),
+                rhs_scale=w_planes[4 * s : P, LAST, n0:n1],
                 start=(s == 0),
                 stop=(s == SUBBANDS - 1),
             )
@@ -269,16 +267,15 @@ def tile_waveletlinearlayer_k_kernel(tc, x, W_words, W_scales, b, out):
             one_pass(LAST, s, 0)
         nc.vector.tensor_tensor(out=result[:, first], in0=acc[0][:], in1=bias[:, first], op=ADD)
         nc.sync.dma_start(out=out[:, first], in_=result[:, first])
-        quarters = []
-        for tag in ("odd_rows", "even_rows"):
-            quarter_bank = bank_pool.tile([P, QUARTER], F32, tag=tag)
-            quarters.append(quarter_bank)
+        ends = []
+        for n0, n1, tag in ((512, 768, "odd_rows"), (768, 896, "even_rows"), (896, 1024, "odd_rows")):
+            end_bank = bank_pool.tile([P, n1 - n0], F32, tag=tag)
+            ends.append((n0, n1, end_bank))
         for s in range(SUBBANDS):
-            for i, bank in enumerate(quarters):
-                last_pass(s, 2 + i, bank)
-        for i, bank in enumerate(quarters):
-            cols = slice((2 + i) * QUARTER, (3 + i) * QUARTER)
+            for n0, n1, bank in ends:
+                last_pass(s, n0, n1, bank)
+        for n0, n1, bank in ends:
             nc.vector.tensor_tensor(
-                out=result[:, cols], in0=bank[:], in1=so_far[:, i * QUARTER : (i + 1) * QUARTER], op=ADD
+                out=result[:, n0:n1], in0=bank[:], in1=so_far[:, n0 - N_TILE : n1 - N_TILE], op=ADD
             )
-            nc.sync.dma_start(out=out[:, cols], in_=result[:, cols])
+            nc.sync.dma_start(out=out[:, n0:n1], in_=result[:, n0:n1])

@@ -69,12 +69,16 @@ def tile_waveletlinearlayer_k_kernel(tc, x, W_words, W_scales, b, out):
         scale_rows = W_scales.rearrange(
             "(ch s h) (q r) n -> ch h q s r n", s=SUBBANDS, h=HALVES, q=QUADRANTS
         )
-        for c in range(CHUNKS):
+
+        def load_scales(queue, word, c, q):
+            queue.dma_start(
+                out=w_planes[32 * q : 32 * q + 16, c, :].bitcast(word),
+                in_=scale_rows[c // HALVES, c % HALVES, q].bitcast(word),
+            )
+
+        for c in range(LAST - 1):
             for q in range(QUADRANTS):
-                nc.gpsimd.dma_start(
-                    out=w_planes[32 * q : 32 * q + 16, c, :].bitcast(F32),
-                    in_=scale_rows[c // HALVES, c % HALVES, q].bitcast(F32),
-                )
+                load_scales(nc.gpsimd, F32, c, q)
 
         chunk_words = W_words.rearrange("(ch s h) p n t -> ch h p s (n t)", s=SUBBANDS, h=HALVES)
         half_bytes = N_TILE * PACK
@@ -99,6 +103,9 @@ def tile_waveletlinearlayer_k_kernel(tc, x, W_words, W_scales, b, out):
                 )
             for s in range(SUBBANDS):
                 w_groups.append(w_chunk[:, s, :])
+            if c < QUADRANTS:
+                for i in (2 * c, 2 * c + 1):
+                    load_scales(nc.sync, I32, LAST - 1 + i // QUADRANTS, i % QUADRANTS)
 
         plus_half = keep.tile([P, P], BF16)
         nc.vector.tensor_scalar_mul(out=plus_half[:], in0=ident[:], scalar1=0.5)

@@ -89,8 +89,8 @@ def tile_waveletlinearlayer_k_kernel(tc, x, W_words, W_scales, b, out):
                 pieces = ((0, 4, 0, 2 * half_bytes),)
             else:
                 pieces = (
-                    (0, 4, 0, half_bytes),
-                    (0, 2, half_bytes, 2 * half_bytes),
+                    (0, 2, 0, 2 * half_bytes),
+                    (2, 4, 0, half_bytes),
                     (2, 3, half_bytes, 2 * half_bytes),
                     (3, 4, half_bytes, 3 * half_bytes // 2),
                     (3, 4, 3 * half_bytes // 2, 7 * half_bytes // 4),
@@ -136,7 +136,8 @@ def tile_waveletlinearlayer_k_kernel(tc, x, W_words, W_scales, b, out):
             )
             sorted_words = work.tile([P, 2, PACK, P], F32)
             for parity in (1, 0):
-                nc.scalar.copy(
+                copy = nc.vector.tensor_copy if c == 0 and parity == 1 else nc.scalar.copy
+                copy(
                     out=sorted_words[:, parity].rearrange("n t (i j) -> n t i j", i=ROWS16),
                     in_=words[:, parity],
                 )
@@ -151,9 +152,11 @@ def tile_waveletlinearlayer_k_kernel(tc, x, W_words, W_scales, b, out):
 
         def halve_odd_rows(c):
             odd_half = ahead.tile([P, PARITY_PIXELS], BF16)
-            nc.scalar.mul(
-                out=odd_half[:], in_=odd_bank_of[c][:].rearrange("p n t -> p (n t)").bitcast(BF16), mul=0.5
-            )
+            odd_pixels = odd_bank_of[c][:].rearrange("p n t -> p (n t)").bitcast(BF16)
+            if c == 0:
+                nc.vector.tensor_scalar_mul(out=odd_half[:], in0=odd_pixels, scalar1=0.5)
+            else:
+                nc.scalar.mul(out=odd_half[:], in_=odd_pixels, mul=0.5)
             odd_half_of[c] = odd_half
 
         def mix_rows(c):

from contextlib import ExitStack

import concourse.mybir as mybir
from concourse.masks import make_identity

BF16 = mybir.dt.bfloat16
F32 = mybir.dt.float32
I32 = mybir.dt.int32
U8 = mybir.dt.uint8
U32 = mybir.dt.uint32
FP8X4 = mybir.dt.float8_e4m3fn_x4
ADD = mybir.AluOpType.add
SUBTRACT = mybir.AluOpType.subtract
MULT = mybir.AluOpType.mult

P = 128
PACK = 4
CHANNELS = 4
SUBBANDS = 4
HALVES = 2
CHUNKS = CHANNELS * HALVES
CHUNK_PIXELS = 2048
PARITY_PIXELS = CHUNK_PIXELS // 2
ROWS16 = 16
J8 = 8
OUT = 1024
N_TILE = 512
N_TILES = OUT // N_TILE
QUADRANTS = 4

FLOPS = 2 * 128 * 16384 * 1024


LEAD = 3
LAST = CHUNKS - 1


def tile_waveletlinearlayer_k_kernel(tc, x, W_words, W_scales, b, out):
    nc = tc.nc
    with ExitStack() as ctx:
        ctx.enter_context(tc.manual_schedule())
        w_pool = ctx.enter_context(tc.tile_pool(name="w_pool", bufs=CHUNKS))
        keep = ctx.enter_context(tc.tile_pool(name="keep", bufs=1))
        work = ctx.enter_context(tc.tile_pool(name="work", bufs=2))
        ahead = ctx.enter_context(tc.tile_pool(name="ahead", bufs=LEAD))
        coded = ctx.enter_context(tc.tile_pool(name="coded", bufs=4))
        acc_pool = ctx.enter_context(tc.psum_pool(name="acc_pool", bufs=1))
        bank_pool = ctx.enter_context(tc.psum_pool(name="bank_pool", bufs=LEAD))

        warm_in = keep.tile([P, 1], F32)
        warm_out = keep.tile([P, 1], F32)
        nc.vector.memset(warm_in[:], 0.0)
        nc.scalar.mul(out=warm_out[:], in_=warm_in[:], mul=0.5)

        ident = keep.tile([P, P], F32)
        make_identity(nc, ident[:])

        w_planes = keep.tile([P, CHUNKS, OUT], U8, align_bytes=64)
        nc.vector.memset(w_planes[:].rearrange("p c n -> p (c n)").bitcast(I32), 0)

        x_chunks = []
        x_all = keep.tile([P, CHUNKS * CHUNK_PIXELS], BF16)
        for c0, c1 in ((0, 1), (1, 4), (4, 8)):
            pixels = slice(c0 * CHUNK_PIXELS, c1 * CHUNK_PIXELS)
            nc.sync.dma_start(out=x_all[:, pixels], in_=x[:, pixels])
        for c in range(CHUNKS):
            x_chunks.append(x_all[:, c * CHUNK_PIXELS : (c + 1) * CHUNK_PIXELS])

        scale_rows = W_scales.rearrange(
            "(ch s h) (q r) n -> ch h q s r n", s=SUBBANDS, h=HALVES, q=QUADRANTS
        )

        def load_scales(queue, word, c, q):
            queue.dma_start(
                out=w_planes[32 * q : 32 * q + 16, c, :].bitcast(word),
                in_=scale_rows[c // HALVES, c % HALVES, q].bitcast(word),
            )

        for c in range(LAST - 1):
            for q in range(QUADRANTS):
                load_scales(nc.gpsimd, F32, c, q)

        chunk_words = W_words.rearrange("(ch s h) p n t -> ch h p s (n t)", s=SUBBANDS, h=HALVES)
        half_bytes = N_TILE * PACK
        w_groups = []
        for c in range(CHUNKS):
            w_chunk = w_pool.tile([P, SUBBANDS, OUT * PACK], U8, align_bytes=64)
            if c < CHUNKS - 1:
                pieces = ((0, 4, 0, 2 * half_bytes),)
            else:
                pieces = (
                    (0, 2, 0, 2 * half_bytes),
                    (2, 4, 0, half_bytes),
                    (2, 3, half_bytes, 2 * half_bytes),
                    (3, 4, half_bytes, 3 * half_bytes // 2),
                    (3, 4, 3 * half_bytes // 2, 7 * half_bytes // 4),
                    (3, 4, 7 * half_bytes // 4, 2 * half_bytes),
                )
            for s0, s1, b0, b1 in pieces:
                nc.sync.dma_start(
                    out=w_chunk[:, s0:s1, b0:b1].bitcast(I32),
                    in_=chunk_words[c // HALVES, c % HALVES][:, s0:s1, b0:b1].bitcast(I32),
                )
            for s in range(SUBBANDS):
                w_groups.append(w_chunk[:, s, :])
            if c < QUADRANTS:
                for i in (2 * c, 2 * c + 1):
                    load_scales(nc.sync, I32, LAST - 1 + i // QUADRANTS, i % QUADRANTS)

        plus_half = keep.tile([P, P], BF16)
        nc.vector.tensor_scalar_mul(out=plus_half[:], in0=ident[:], scalar1=0.5)
        minus_half = keep.tile([P, P], BF16)
        nc.vector.tensor_scalar_mul(out=minus_half[:], in0=ident[:], scalar1=-0.5)
        ones = keep.tile([P, P], BF16)
        nc.vector.memset(ones[:], 1.0)
        bias_rows = keep.tile([P, OUT], BF16)
        nc.vector.memset(bias_rows[:], 0.0)
        nc.scalar.dma_start(out=bias_rows[0:1, :], in_=b.rearrange("(o n) -> o n", o=1))

        acc = []
        for half in range(N_TILES):
            acc_bank = acc_pool.tile([P, N_TILE], F32, name="acc%d" % half)
            acc.append(acc_bank)

        sorted_of = {}
        odd_bank_of = {}
        even_bank_of = {}
        odd_half_of = {}
        row_mix_of = {}
        codes_of = {}
        scales_of = {}

        def sort_and_transpose(c):
            words = x_chunks[c].bitcast(F32).rearrange(
                "n (i a j t) -> n a t i j", i=ROWS16, a=2, j=J8, t=PACK
            )
            sorted_words = work.tile([P, 2, PACK, P], F32)
            for parity in (1, 0):
                copy = nc.vector.tensor_copy if c == 0 and parity == 1 else nc.scalar.copy
                copy(
                    out=sorted_words[:, parity].rearrange("n t (i j) -> n t i j", i=ROWS16),
                    in_=words[:, parity],
                )
            odd_rows = bank_pool.tile([P, P, PACK], F32, tag="odd_rows")
            even_rows = bank_pool.tile([P, P, PACK], F32, tag="even_rows")
            for t4 in range(PACK):
                nc.tensor.transpose(out=odd_rows[:, :, t4], in_=sorted_words[:, 1, t4, :], identity=ident[:])
            for t4 in range(PACK):
                nc.tensor.transpose(out=even_rows[:, :, t4], in_=sorted_words[:, 0, t4, :], identity=ident[:])
            odd_bank_of[c] = odd_rows
            even_bank_of[c] = even_rows

        def halve_odd_rows(c):
            odd_half = ahead.tile([P, PARITY_PIXELS], BF16)
            odd_pixels = odd_bank_of[c][:].rearrange("p n t -> p (n t)").bitcast(BF16)
            if c == 0:
                nc.vector.tensor_scalar_mul(out=odd_half[:], in0=odd_pixels, scalar1=0.5)
            else:
                nc.scalar.mul(out=odd_half[:], in_=odd_pixels, mul=0.5)
            odd_half_of[c] = odd_half

        def mix_rows(c):
            even_pixels = even_bank_of[c][:].rearrange("p n t -> p (n t)").bitcast(BF16)
            row_mix = work.tile([P, 2, PARITY_PIXELS], F32)
            nc.vector.scalar_tensor_tensor(
                out=row_mix[:, 0, :], in0=even_pixels, scalar=0.5, in1=odd_half_of[c][:], op0=MULT, op1=ADD
            )
            nc.vector.scalar_tensor_tensor(
                out=row_mix[:, 1, :], in0=even_pixels, scalar=0.5, in1=odd_half_of[c][:], op0=MULT, op1=SUBTRACT
            )
            row_mix_of[c] = row_mix

        def mix_columns_and_quantise(c):
            pixels = row_mix_of[c][:].rearrange("p m (n t e) -> p e m n t", t=PACK, n=P, e=2)
            sums = work.tile([P, 2, P, PACK], BF16, align_bytes=64)
            differences = work.tile([P, 2, P, PACK], BF16, align_bytes=64)
            nc.vector.tensor_tensor(out=sums[:], in0=pixels[:, 0], in1=pixels[:, 1], op=ADD)
            nc.vector.tensor_tensor(out=differences[:], in0=pixels[:, 0], in1=pixels[:, 1], op=SUBTRACT)
            for pair, features in enumerate((sums, differences)):
                quantise(c, pair, features[:].rearrange("p m n t -> p (m n t)"))

        def quantise(c, pair, features):
            t_codes = coded.tile([P, 2 * P], U32, align_bytes=64, name="t_codes%d" % pair)
            t_scales = coded.tile([P, 2 * P], U8, align_bytes=64, name="t_scales%d" % pair)
            nc.vector.quantize_mx(out=t_codes[:].bitcast(FP8X4), scales=t_scales[:], in_=features)
            codes_of[(c, pair)] = t_codes
            scales_of[(c, pair)] = t_scales

        last_pixels = keep.tile([P, 2, PARITY_PIXELS], BF16)
        last_features = keep.tile([P, SUBBANDS, N_TILE], BF16, align_bytes=64)

        def fetch_pixels(c):
            for parity, bank in ((1, odd_bank_of[c]), (0, even_bank_of[c])):
                nc.scalar.copy(
                    out=last_pixels[:, parity, :], in_=bank[:].rearrange("p n t -> p (n t)").bitcast(BF16)
                )

        def transform(pair):
            for s, tag in ((2 * pair, "odd_rows"), (2 * pair + 1, "even_rows")):
                feature_bank = bank_pool.tile([P, N_TILE], F32, tag=tag)
                for a in range(2):
                    for e in range(2):
                        negative = (a * (s % 2) + e * (s // 2)) % 2 == 1
                        nc.tensor.matmul(
                            out=feature_bank[:],
                            lhsT=(minus_half if negative else plus_half)[:],
                            rhs=last_pixels[:, a, :].rearrange("p (w e) -> p e w", e=2)[:, e, :],
                            start=(a == 0 and e == 0),
                            stop=(a == 1 and e == 1),
                        )
                nc.scalar.copy(out=last_features[:, s, :], in_=feature_bank[:])

        def last_pass(s, n0, n1, bank):
            batch_cols = slice(s % 2 * P, (s % 2 + 1) * P)
            nc.tensor.matmul_mx(
                out=bank[:],
                lhsT=codes_of[(LAST, s // 2)][:, batch_cols].bitcast(FP8X4),
                lhsT_scale=scales_of[(LAST, s // 2)][:, batch_cols],
                rhs=w_groups[LAST * SUBBANDS + s][:, n0 * PACK : n1 * PACK].bitcast(FP8X4),
                rhs_scale=w_planes[4 * s : P, LAST, n0:n1],
                start=(s == 0),
                stop=(s == SUBBANDS - 1),
            )

        def one_pass(c, s, half):
            batch_cols = slice(s % 2 * P, (s % 2 + 1) * P)
            nc.tensor.matmul_mx(
                out=acc[half][:],
                lhsT=codes_of[(c, s // 2)][:, batch_cols].bitcast(FP8X4),
                lhsT_scale=scales_of[(c, s // 2)][:, batch_cols],
                rhs=w_groups[c * SUBBANDS + s][:, half * N_TILE * PACK : (half + 1) * N_TILE * PACK].bitcast(FP8X4),
                rhs_scale=w_planes[4 * s : P, c, half * N_TILE : (half + 1) * N_TILE],
                start=(c == 0 and s == 0),
                stop=(c == CHUNKS - 1 - half and s == SUBBANDS - 1),
            )

        def multiply(c):
            for s in range(SUBBANDS):
                for half in range(N_TILES):
                    one_pass(c, s, half)

        for c in range(LEAD):
            sort_and_transpose(c)
            if c < LEAD - 1:
                halve_odd_rows(c)
        for c in range(LAST):
            mix_rows(c)
            if c + LEAD < CHUNKS:
                sort_and_transpose(c + LEAD)
            if c + LEAD - 1 < LAST:
                halve_odd_rows(c + LEAD - 1)
            if c + LEAD == LAST:
                fetch_pixels(LAST)
            if c >= LAST - 2:
                transform(c - (LAST - 2))
            if c >= 1:
                mix_columns_and_quantise(c - 1)
                multiply(c - 1)

        bias = keep.tile([P, OUT], F32)
        for half in range(N_TILES):
            cols = slice(half * N_TILE, (half + 1) * N_TILE)
            bias_bank = bank_pool.tile([P, N_TILE], F32, tag="even_rows")
            nc.tensor.matmul(out=bias_bank[:], lhsT=ones[:], rhs=bias_rows[:, cols], start=True, stop=True)
            nc.scalar.copy(out=bias[:, cols], in_=bias_bank[:])

        mix_columns_and_quantise(LAST - 1)
        multiply(LAST - 1)
        for pair in range(2):
            quantise(LAST, pair, last_features[:, 2 * pair : 2 * pair + 2, :].rearrange("p m c -> p (m c)"))

        result = keep.tile([P, OUT], F32)
        so_far = keep.tile([P, N_TILE], F32)
        first, second = slice(0, N_TILE), slice(N_TILE, OUT)
        nc.vector.tensor_tensor(out=so_far[:], in0=acc[1][:], in1=bias[:, second], op=ADD)
        for s in range(SUBBANDS):
            one_pass(LAST, s, 0)
        nc.vector.tensor_tensor(out=result[:, first], in0=acc[0][:], in1=bias[:, first], op=ADD)
        nc.sync.dma_start(out=out[:, first], in_=result[:, first])
        ends = []
        for n0, n1, tag in ((512, 768, "odd_rows"), (768, 896, "even_rows"), (896, 1024, "odd_rows")):
            end_bank = bank_pool.tile([P, n1 - n0], F32, tag=tag)
            ends.append((n0, n1, end_bank))
        for s in range(SUBBANDS):
            for n0, n1, bank in ends:
                last_pass(s, n0, n1, bank)
        for n0, n1, bank in ends:
            nc.vector.tensor_tensor(
                out=result[:, n0:n1], in0=bank[:], in1=so_far[:, n0 - N_TILE : n1 - N_TILE], op=ADD
            )
            nc.sync.dma_start(out=out[:, n0:n1], in_=result[:, n0:n1])
